import numpy as np
import ml_dtypes


def mxq(x, axis, fmt="e4m3"):
    dtype, down = {"e4m3": (ml_dtypes.float8_e4m3fn, 7), "e5m2": (ml_dtypes.float8_e5m2, 14)}[fmt]
    v = np.moveaxis(np.asarray(x, np.float32).astype(ml_dtypes.bfloat16).astype(np.float64), axis, -1)
    blocks = v.reshape(v.shape[:-1] + (-1, 32))
    amax = np.abs(blocks).max(-1, keepdims=True)
    byte = np.maximum(np.where(amax > 0, np.frexp(amax)[1] - 1 + 127, 0) - down, 1)
    scale = np.exp2(byte - 127.0)
    codes = (blocks / scale).astype(np.float32).astype(dtype).astype(np.float64)
    return np.moveaxis((codes * scale).reshape(v.shape), -1, axis)


WIDE = False


def mx_kscale(k):
    if not WIDE:
        return np.ones(k)
    levels = np.array([10, -10, 5, -5, 0])
    a = np.random.permutation(np.resize(levels, k // 512 * 4)).reshape(k // 512, 4)
    idx = np.arange(k)
    return np.exp2(a[idx // 512, idx % 128 // 32])


BF16 = ml_dtypes.bfloat16


def bf(x):
    return np.asarray(x, np.float32).astype(BF16)


def f64(x):
    return np.asarray(x).astype(np.float64)


B, S, H, NH, HD = 4, 2048, 1024, 2, 64
E = NH * HD
HALF = HD // 2


def rope_tables():
    inv_freq = 1.0 / 10000.0 ** (np.arange(0, HD, 2) / HD)
    pos = np.random.randint(0, S) + np.arange(S)
    freqs = np.outer(pos, inv_freq)
    emb = np.concatenate([freqs, freqs], axis=-1)
    return bf(np.cos(emb)), bf(np.sin(emb))


def apply_rotary(x, cos, sin):
    c = cos[None, None, :, :]
    s = sin[None, None, :, :]
    x1, x2 = x[..., :HALF], x[..., HALF:]
    rotated = np.concatenate([-x2, x1], axis=-1)
    return x * c + rotated * s


def setup_inputs():
    s = mx_kscale(H)
    cos, sin = rope_tables()
    return {"hidden_states": bf(np.random.standard_normal((B, S, H)) * s),
            "cos": cos, "sin": sin,
            "w_qkv": bf(np.random.standard_normal((3 * E, H)) / np.sqrt(H) / s[None, :])}


def reference(hidden_states, cos, sin, w_qkv):
    qkv = mxq(f64(hidden_states), 2, "e4m3") @ mxq(f64(w_qkv), 1, "e4m3").T
    qkv = qkv.reshape(B, S, 3, NH, HD).transpose(2, 0, 3, 1, 4)
    q, k, v = qkv[0], qkv[1], qkv[2]
    q = apply_rotary(q, f64(cos), f64(sin))
    k = apply_rotary(k, f64(cos), f64(sin))
    return q, k, v

@@ -1,0 +1,190 @@
+from contextlib import ExitStack
+
+import concourse.mybir as mybir
+from concourse.masks import make_identity
+
+BF16 = mybir.dt.bfloat16
+F32 = mybir.dt.float32
+U32 = mybir.dt.uint32
+U8 = mybir.dt.uint8
+FP8X4 = mybir.dt.float8_e4m3fn_x4
+MULT = mybir.AluOpType.mult
+ADD = mybir.AluOpType.add
+
+B, S, H, NH, HD = 4, 2048, 1024, 2, 64
+E = NH * HD
+HALF = HD // 2
+P = 128
+PACK = 4
+PASSES = H // (P * PACK)
+ROW_WORDS = H // 2
+WORD_BLOCKS = ROW_WORDS // P
+POS = S // P
+ROUND_TILES = 4
+ROUNDS_PER_BATCH = POS // ROUND_TILES
+ROUNDS = B * ROUNDS_PER_BATCH
+STORE_TILES = 8
+LOOKAHEAD = 5
+
+FLOPS = 2 * B * S * H * 3 * E
+
+
+def tile_flashattention_pa_t_kernel(tc, hidden_states, cos, sin, w_qkv, out_0, out_1, out_2):
+    nc = tc.nc
+    outs = (out_0, out_1, out_2)
+
+    with ExitStack() as ctx:
+        const = ctx.enter_context(tc.tile_pool(name="const", bufs=1))
+        x_pool = ctx.enter_context(tc.tile_pool(name="x", bufs=LOOKAHEAD))
+        grouped_pool = ctx.enter_context(tc.tile_pool(name="grouped", bufs=4))
+        code_pool = ctx.enter_context(tc.tile_pool(name="codes", bufs=3))
+        sin_pool = ctx.enter_context(tc.tile_pool(name="sin_part", bufs=3))
+        res_pool = ctx.enter_context(tc.tile_pool(name="res", bufs=3))
+        xt_pool = ctx.enter_context(tc.psum_pool(name="xt", bufs=4))
+        qk_pool = ctx.enter_context(tc.psum_pool(name="qk", bufs=2))
+        v_pool = ctx.enter_context(tc.psum_pool(name="v", bufs=2))
+
+        def transpose_rows(words):
+            xt = xt_pool.tile([P, WORD_BLOCKS, P], F32)
+            for blk in range(WORD_BLOCKS):
+                nc.tensor.transpose(xt[:, blk, :], words[:, blk * P : (blk + 1) * P], ident[:])
+            return xt
+
+        def regroup(dst_words, xt):
+            nc.scalar.copy(out=dst_words, in_=xt[:].rearrange("p (g u) r -> p g r u", u=2))
+
+        ident = const.tile([P, P], F32)
+        make_identity(nc, ident[:])
+
+        w_sb = const.tile([P, 3 * H], BF16)
+        nc.sync.dma_start(
+            out=w_sb[:].rearrange("p (a k) -> p a k", a=3), in_=w_qkv.rearrange("(a p) k -> p a k", p=P)
+        )
+
+        def load_round(r):
+            b, quarter = divmod(r, ROUNDS_PER_BATCH)
+            x_sb = x_pool.tile([P, ROUND_TILES * H], BF16)
+            rows = hidden_states[b].rearrange("(p j) k -> p (j k)", j=POS)
+            nc.sync.dma_start(out=x_sb[:], in_=rows[:, quarter * ROUND_TILES * H : (quarter + 1) * ROUND_TILES * H])
+            return x_sb
+
+        x_tiles = {}
+        x_tiles[0] = load_round(0)
+
+        cos_sb = const.tile([P, POS, HD], BF16)
+        sin_sb = const.tile([P, POS, HD], BF16)
+        nc.sync.dma_start(out=cos_sb[:], in_=cos.rearrange("(p j) d -> p j d", j=POS))
+        nc.sync.dma_start(out=sin_sb[:], in_=sin.rearrange("(p j) d -> p j d", j=POS))
+        nc.vector.tensor_scalar_mul(out=sin_sb[:, :, 0:HALF], in0=sin_sb[:, :, 0:HALF], scalar1=-1.0)
+
+        for r in range(1, LOOKAHEAD):
+            x_tiles[r] = load_round(r)
+
+        w_words = w_sb[:].bitcast(F32).rearrange("p (a w) -> p a w", a=3)
+        w_grouped = const.tile([P, PASSES * 3 * E * PACK], BF16, align_bytes=64)
+        w_grouped_words = w_grouped[:].bitcast(F32).rearrange("p (g a n u) -> p g a n u", g=PASSES, a=3, u=2)
+        for a in range(3):
+            regroup(w_grouped_words[:, :, a, :, :], transpose_rows(w_words[:, a, :]))
+        w_codes = const.tile([P, PASSES * 3 * E], U32, align_bytes=64)
+        w_scales = const.tile([P, PASSES * 3 * E], U8, align_bytes=64)
+        QK_COLS = (0, 2 * E)
+        V_COLS = (2 * E, 3 * E)
+
+        def w_cols(g, cols):
+            return slice(g * 3 * E + cols[0], g * 3 * E + cols[1])
+
+        for g in range(PASSES):
+            for cols in (QK_COLS, V_COLS):
+                nc.vector.quantize_mx(
+                    out=w_codes[:, w_cols(g, cols)].bitcast(FP8X4),
+                    scales=w_scales[:, w_cols(g, cols)],
+                    in_=w_grouped[:, (g * 3 * E + cols[0]) * PACK : (g * 3 * E + cols[1]) * PACK],
+                )
+
+        def transpose_and_quantise(x_sb):
+            x_words = x_sb[:].bitcast(F32).rearrange("p (t w) -> p t w", t=ROUND_TILES)
+            x_codes = code_pool.tile([P, ROUND_TILES * PASSES * P], U32, align_bytes=64)
+            x_scales = code_pool.tile([P, ROUND_TILES * PASSES * P], U8, align_bytes=64)
+            banks = [transpose_rows(x_words[:, t, :]) for t in range(ROUND_TILES)]
+            for pair in range(ROUND_TILES // 2):
+                grouped = grouped_pool.tile([P, 2 * PASSES * P * PACK], BF16, align_bytes=64)
+                grouped_words = grouped[:].bitcast(F32).rearrange("p (t g r u) -> p t g r u", t=2, g=PASSES, u=2)
+                for i in range(2):
+                    regroup(grouped_words[:, i], banks[2 * pair + i])
+                cols = slice(pair * 2 * PASSES * P, (pair + 1) * 2 * PASSES * P)
+                nc.vector.quantize_mx(out=x_codes[:, cols].bitcast(FP8X4), scales=x_scales[:, cols], in_=grouped[:])
+            return x_codes, x_scales
+
+        def multiply(x_codes, x_scales):
+            v_ps = v_pool.tile([P, ROUND_TILES, E], F32)
+            qk_banks = []
+            for pair in range(ROUND_TILES // 2):
+                qk_ps = qk_pool.tile([P, 2, 2 * E], F32)
+                qk_banks.append(qk_ps)
+                for i in range(2):
+                    t = 2 * pair + i
+                    for g in range(PASSES):
+                        tokens = slice((t * PASSES + g) * P, (t * PASSES + g + 1) * P)
+                        for acc, cols in ((qk_ps[:, i, :], QK_COLS), (v_ps[:, t, :], V_COLS)):
+                            nc.tensor.matmul_mx(
+                                out=acc,
+                                lhsT=x_codes[:, tokens].bitcast(FP8X4),
+                                lhsT_scale=x_scales[:, tokens],
+                                rhs=w_codes[:, w_cols(g, cols)].bitcast(FP8X4),
+                                rhs_scale=w_scales[:, w_cols(g, cols)],
+                                start=(g == 0),
+                                stop=(g == PASSES - 1),
+                            )
+            return qk_banks, v_ps
+
+        def rotate(first_pos, qk_banks, v_ps, res_view, slot):
+            sin_part = sin_pool.tile([P, 2 * NH, ROUND_TILES, HD], F32)
+            for pair in range(ROUND_TILES // 2):
+                x = qk_banks[pair][:].rearrange("p t (c d) -> p t c d", d=HD)
+                js = slice(first_pos + 2 * pair, first_pos + 2 * pair + 2)
+                ts = slice(2 * pair, 2 * pair + 2)
+                nc.vector.tensor_tensor(
+                    out=res_view[:, 0 : 2 * NH, slot + 2 * pair : slot + 2 * pair + 2, :].rearrange("p c t d -> p t c d"),
+                    in0=x,
+                    in1=cos_sb[:, js, :].unsqueeze(2).to_broadcast([P, 2, 2 * NH, HD]),
+                    op=MULT,
+                )
+                for dst, src in ((slice(0, HALF), slice(HALF, HD)), (slice(HALF, HD), slice(0, HALF))):
+                    nc.vector.tensor_tensor(
+                        out=sin_part[:, :, ts, dst].rearrange("p c t d -> p t c d"),
+                        in0=x[:, :, :, src],
+                        in1=sin_sb[:, js, dst].unsqueeze(2).to_broadcast([P, 2, 2 * NH, HALF]),
+                        op=MULT,
+                    )
+            rotated = res_view[:, 0 : 2 * NH, slot : slot + ROUND_TILES, :]
+            nc.gpsimd.tensor_tensor(out=rotated, in0=rotated, in1=sin_part[:], op=ADD)
+            nc.scalar.copy(
+                out=res_view[:, 2 * NH : 3 * NH, slot : slot + ROUND_TILES, :],
+                in_=v_ps[:].rearrange("p t (h d) -> p h t d", d=HD),
+            )
+
+        def store(b, first_pos, res_view):
+            for which in range(3):
+                rows = outs[which][b].rearrange("h (p j) d -> p h j d", j=POS)
+                nc.sync.dma_start(
+                    out=rows[:, :, first_pos : first_pos + STORE_TILES, :],
+                    in_=res_view[:, which * NH : (which + 1) * NH, :, :],
+                )
+
+        quantised = {0: transpose_and_quantise(x_tiles[0])}
+        res_view = None
+        for r in range(ROUNDS):
+            b, quarter = divmod(r, ROUNDS_PER_BATCH)
+            first_pos = quarter * ROUND_TILES
+            slot = first_pos % STORE_TILES
+            if r + LOOKAHEAD < ROUNDS:
+                x_tiles[r + LOOKAHEAD] = load_round(r + LOOKAHEAD)
+            if r + 1 < ROUNDS:
+                quantised[r + 1] = transpose_and_quantise(x_tiles[r + 1])
+            qk_banks, v_ps = multiply(quantised[r][0], quantised[r][1])
+            if slot == 0:
+                res = res_pool.tile([P, 3 * NH, STORE_TILES, HD], F32)
+                res_view = res[:]
+            rotate(first_pos, qk_banks, v_ps, res_view, slot)
+            if slot + ROUND_TILES == STORE_TILES:
+                store(b, first_pos + ROUND_TILES - STORE_TILES, res_view)

@@ -34,6 +34,7 @@ def tile_flashattention_pa_t_kernel(tc, hidden_states, cos, sin, w_qkv, out_0, o
     outs = (out_0, out_1, out_2)
 
     with ExitStack() as ctx:
+        ctx.enter_context(tc.manual_schedule())
         const = ctx.enter_context(tc.tile_pool(name="const", bufs=1))
         x_pool = ctx.enter_context(tc.tile_pool(name="x", bufs=LOOKAHEAD))
         grouped_pool = ctx.enter_context(tc.tile_pool(name="grouped", bufs=4))

@@ -158,7 +158,7 @@ def tile_flashattention_pa_t_kernel(tc, hidden_states, cos, sin, w_qkv, out_0, o
                         op=MULT,
                     )
             rotated = res_view[:, 0 : 2 * NH, slot : slot + ROUND_TILES, :]
-            nc.gpsimd.tensor_tensor(out=rotated, in0=rotated, in1=sin_part[:], op=ADD)
+            nc.vector.tensor_tensor(out=rotated, in0=rotated, in1=sin_part[:], op=ADD)
             nc.scalar.copy(
                 out=res_view[:, 2 * NH : 3 * NH, slot : slot + ROUND_TILES, :],
                 in_=v_ps[:].rearrange("p t (h d) -> p h t d", d=HD),

@@ -37,7 +37,7 @@ def tile_flashattention_pa_t_kernel(tc, hidden_states, cos, sin, w_qkv, out_0, o
         ctx.enter_context(tc.manual_schedule())
         const = ctx.enter_context(tc.tile_pool(name="const", bufs=1))
         x_pool = ctx.enter_context(tc.tile_pool(name="x", bufs=LOOKAHEAD))
-        grouped_pool = ctx.enter_context(tc.tile_pool(name="grouped", bufs=4))
+        grouped_pool = ctx.enter_context(tc.tile_pool(name="grouped", bufs=6))
         code_pool = ctx.enter_context(tc.tile_pool(name="codes", bufs=3))
         sin_pool = ctx.enter_context(tc.tile_pool(name="sin_part", bufs=3))
         res_pool = ctx.enter_context(tc.tile_pool(name="res", bufs=3))
@@ -102,18 +102,26 @@ def tile_flashattention_pa_t_kernel(tc, hidden_states, cos, sin, w_qkv, out_0, o
                     in_=w_grouped[:, (g * 3 * E + cols[0]) * PACK : (g * 3 * E + cols[1]) * PACK],
                 )
 
-        def transpose_and_quantise(x_sb):
+        def transpose_round(x_sb):
             x_words = x_sb[:].bitcast(F32).rearrange("p (t w) -> p t w", t=ROUND_TILES)
-            x_codes = code_pool.tile([P, ROUND_TILES * PASSES * P], U32, align_bytes=64)
-            x_scales = code_pool.tile([P, ROUND_TILES * PASSES * P], U8, align_bytes=64)
             banks = [transpose_rows(x_words[:, t, :]) for t in range(ROUND_TILES)]
+            grouped_pairs = []
             for pair in range(ROUND_TILES // 2):
                 grouped = grouped_pool.tile([P, 2 * PASSES * P * PACK], BF16, align_bytes=64)
                 grouped_words = grouped[:].bitcast(F32).rearrange("p (t g r u) -> p t g r u", t=2, g=PASSES, u=2)
                 for i in range(2):
                     regroup(grouped_words[:, i], banks[2 * pair + i])
+                grouped_pairs.append(grouped)
+            return grouped_pairs
+
+        def quantise_round(grouped_pairs):
+            x_codes = code_pool.tile([P, ROUND_TILES * PASSES * P], U32, align_bytes=64)
+            x_scales = code_pool.tile([P, ROUND_TILES * PASSES * P], U8, align_bytes=64)
+            for pair in range(ROUND_TILES // 2):
                 cols = slice(pair * 2 * PASSES * P, (pair + 1) * 2 * PASSES * P)
-                nc.vector.quantize_mx(out=x_codes[:, cols].bitcast(FP8X4), scales=x_scales[:, cols], in_=grouped[:])
+                nc.vector.quantize_mx(
+                    out=x_codes[:, cols].bitcast(FP8X4), scales=x_scales[:, cols], in_=grouped_pairs[pair][:]
+                )
             return x_codes, x_scales
 
         def multiply(x_codes, x_scales):
@@ -158,7 +166,7 @@ def tile_flashattention_pa_t_kernel(tc, hidden_states, cos, sin, w_qkv, out_0, o
                         op=MULT,
                     )
             rotated = res_view[:, 0 : 2 * NH, slot : slot + ROUND_TILES, :]
-            nc.vector.tensor_tensor(out=rotated, in0=rotated, in1=sin_part[:], op=ADD)
+            nc.gpsimd.tensor_tensor(out=rotated, in0=rotated, in1=sin_part[:], op=ADD)
             nc.scalar.copy(
                 out=res_view[:, 2 * NH : 3 * NH, slot : slot + ROUND_TILES, :],
                 in_=v_ps[:].rearrange("p t (h d) -> p h t d", d=HD),
@@ -172,7 +180,8 @@ def tile_flashattention_pa_t_kernel(tc, hidden_states, cos, sin, w_qkv, out_0, o
                     in_=res_view[:, which * NH : (which + 1) * NH, :, :],
                 )
 
-        quantised = {0: transpose_and_quantise(x_tiles[0])}
+        grouped_rounds = {0: transpose_round(x_tiles[0]), 1: transpose_round(x_tiles[1])}
+        quantised = {0: quantise_round(grouped_rounds[0])}
         res_view = None
         for r in range(ROUNDS):
             b, quarter = divmod(r, ROUNDS_PER_BATCH)
@@ -180,8 +189,10 @@ def tile_flashattention_pa_t_kernel(tc, hidden_states, cos, sin, w_qkv, out_0, o
             slot = first_pos % STORE_TILES
             if r + LOOKAHEAD < ROUNDS:
                 x_tiles[r + LOOKAHEAD] = load_round(r + LOOKAHEAD)
+            if r + 2 < ROUNDS:
+                grouped_rounds[r + 2] = transpose_round(x_tiles[r + 2])
             if r + 1 < ROUNDS:
-                quantised[r + 1] = transpose_and_quantise(x_tiles[r + 1])
+                quantised[r + 1] = quantise_round(grouped_rounds[r + 1])
             qk_banks, v_ps = multiply(quantised[r][0], quantised[r][1])
             if slot == 0:
                 res = res_pool.tile([P, 3 * NH, STORE_TILES, HD], F32)

@@ -154,15 +154,15 @@ def tile_flashattention_pa_t_kernel(tc, hidden_states, cos, sin, w_qkv, out_0, o
                 ts = slice(2 * pair, 2 * pair + 2)
                 nc.vector.tensor_tensor(
                     out=res_view[:, 0 : 2 * NH, slot + 2 * pair : slot + 2 * pair + 2, :].rearrange("p c t d -> p t c d"),
-                    in0=x,
-                    in1=cos_sb[:, js, :].unsqueeze(2).to_broadcast([P, 2, 2 * NH, HD]),
+                    in0=cos_sb[:, js, :].unsqueeze(2).to_broadcast([P, 2, 2 * NH, HD]),
+                    in1=x,
                     op=MULT,
                 )
                 for dst, src in ((slice(0, HALF), slice(HALF, HD)), (slice(HALF, HD), slice(0, HALF))):
                     nc.vector.tensor_tensor(
                         out=sin_part[:, :, ts, dst].rearrange("p c t d -> p t c d"),
-                        in0=x[:, :, :, src],
-                        in1=sin_sb[:, js, dst].unsqueeze(2).to_broadcast([P, 2, 2 * NH, HALF]),
+                        in0=sin_sb[:, js, dst].unsqueeze(2).to_broadcast([P, 2, 2 * NH, HALF]),
+                        in1=x[:, :, :, src],
                         op=MULT,
                     )
             rotated = res_view[:, 0 : 2 * NH, slot : slot + ROUND_TILES, :]

from contextlib import ExitStack

import concourse.mybir as mybir
from concourse.masks import make_identity

BF16 = mybir.dt.bfloat16
F32 = mybir.dt.float32
U32 = mybir.dt.uint32
U8 = mybir.dt.uint8
FP8X4 = mybir.dt.float8_e4m3fn_x4
MULT = mybir.AluOpType.mult
ADD = mybir.AluOpType.add

B, S, H, NH, HD = 4, 2048, 1024, 2, 64
E = NH * HD
HALF = HD // 2
P = 128
PACK = 4
PASSES = H // (P * PACK)
ROW_WORDS = H // 2
WORD_BLOCKS = ROW_WORDS // P
POS = S // P
ROUND_TILES = 4
ROUNDS_PER_BATCH = POS // ROUND_TILES
ROUNDS = B * ROUNDS_PER_BATCH
STORE_TILES = 8
LOOKAHEAD = 5

FLOPS = 2 * B * S * H * 3 * E


def tile_flashattention_pa_t_kernel(tc, hidden_states, cos, sin, w_qkv, out_0, out_1, out_2):
    nc = tc.nc
    outs = (out_0, out_1, out_2)

    with ExitStack() as ctx:
        ctx.enter_context(tc.manual_schedule())
        const = ctx.enter_context(tc.tile_pool(name="const", bufs=1))
        x_pool = ctx.enter_context(tc.tile_pool(name="x", bufs=LOOKAHEAD))
        grouped_pool = ctx.enter_context(tc.tile_pool(name="grouped", bufs=6))
        code_pool = ctx.enter_context(tc.tile_pool(name="codes", bufs=3))
        sin_pool = ctx.enter_context(tc.tile_pool(name="sin_part", bufs=3))
        res_pool = ctx.enter_context(tc.tile_pool(name="res", bufs=3))
        xt_pool = ctx.enter_context(tc.psum_pool(name="xt", bufs=4))
        qk_pool = ctx.enter_context(tc.psum_pool(name="qk", bufs=2))
        v_pool = ctx.enter_context(tc.psum_pool(name="v", bufs=2))

        def transpose_rows(words):
            xt = xt_pool.tile([P, WORD_BLOCKS, P], F32)
            for blk in range(WORD_BLOCKS):
                nc.tensor.transpose(xt[:, blk, :], words[:, blk * P : (blk + 1) * P], ident[:])
            return xt

        def regroup(dst_words, xt):
            nc.scalar.copy(out=dst_words, in_=xt[:].rearrange("p (g u) r -> p g r u", u=2))

        ident = const.tile([P, P], F32)
        make_identity(nc, ident[:])

        w_sb = const.tile([P, 3 * H], BF16)
        nc.sync.dma_start(
            out=w_sb[:].rearrange("p (a k) -> p a k", a=3), in_=w_qkv.rearrange("(a p) k -> p a k", p=P)
        )

        def load_round(r):
            b, quarter = divmod(r, ROUNDS_PER_BATCH)
            x_sb = x_pool.tile([P, ROUND_TILES * H], BF16)
            rows = hidden_states[b].rearrange("(p j) k -> p (j k)", j=POS)
            nc.sync.dma_start(out=x_sb[:], in_=rows[:, quarter * ROUND_TILES * H : (quarter + 1) * ROUND_TILES * H])
            return x_sb

        x_tiles = {}
        x_tiles[0] = load_round(0)

        cos_sb = const.tile([P, POS, HD], BF16)
        sin_sb = const.tile([P, POS, HD], BF16)
        nc.sync.dma_start(out=cos_sb[:], in_=cos.rearrange("(p j) d -> p j d", j=POS))
        nc.sync.dma_start(out=sin_sb[:], in_=sin.rearrange("(p j) d -> p j d", j=POS))
        nc.vector.tensor_scalar_mul(out=sin_sb[:, :, 0:HALF], in0=sin_sb[:, :, 0:HALF], scalar1=-1.0)

        for r in range(1, LOOKAHEAD):
            x_tiles[r] = load_round(r)

        w_words = w_sb[:].bitcast(F32).rearrange("p (a w) -> p a w", a=3)
        w_grouped = const.tile([P, PASSES * 3 * E * PACK], BF16, align_bytes=64)
        w_grouped_words = w_grouped[:].bitcast(F32).rearrange("p (g a n u) -> p g a n u", g=PASSES, a=3, u=2)
        for a in range(3):
            regroup(w_grouped_words[:, :, a, :, :], transpose_rows(w_words[:, a, :]))
        w_codes = const.tile([P, PASSES * 3 * E], U32, align_bytes=64)
        w_scales = const.tile([P, PASSES * 3 * E], U8, align_bytes=64)
        QK_COLS = (0, 2 * E)
        V_COLS = (2 * E, 3 * E)

        def w_cols(g, cols):
            return slice(g * 3 * E + cols[0], g * 3 * E + cols[1])

        for g in range(PASSES):
            for cols in (QK_COLS, V_COLS):
                nc.vector.quantize_mx(
                    out=w_codes[:, w_cols(g, cols)].bitcast(FP8X4),
                    scales=w_scales[:, w_cols(g, cols)],
                    in_=w_grouped[:, (g * 3 * E + cols[0]) * PACK : (g * 3 * E + cols[1]) * PACK],
                )

        def transpose_round(x_sb):
            x_words = x_sb[:].bitcast(F32).rearrange("p (t w) -> p t w", t=ROUND_TILES)
            banks = [transpose_rows(x_words[:, t, :]) for t in range(ROUND_TILES)]
            grouped_pairs = []
            for pair in range(ROUND_TILES // 2):
                grouped = grouped_pool.tile([P, 2 * PASSES * P * PACK], BF16, align_bytes=64)
                grouped_words = grouped[:].bitcast(F32).rearrange("p (t g r u) -> p t g r u", t=2, g=PASSES, u=2)
                for i in range(2):
                    regroup(grouped_words[:, i], banks[2 * pair + i])
                grouped_pairs.append(grouped)
            return grouped_pairs

        def quantise_round(grouped_pairs):
            x_codes = code_pool.tile([P, ROUND_TILES * PASSES * P], U32, align_bytes=64)
            x_scales = code_pool.tile([P, ROUND_TILES * PASSES * P], U8, align_bytes=64)
            for pair in range(ROUND_TILES // 2):
                cols = slice(pair * 2 * PASSES * P, (pair + 1) * 2 * PASSES * P)
                nc.vector.quantize_mx(
                    out=x_codes[:, cols].bitcast(FP8X4), scales=x_scales[:, cols], in_=grouped_pairs[pair][:]
                )
            return x_codes, x_scales

        def multiply(x_codes, x_scales):
            v_ps = v_pool.tile([P, ROUND_TILES, E], F32)
            qk_banks = []
            for pair in range(ROUND_TILES // 2):
                qk_ps = qk_pool.tile([P, 2, 2 * E], F32)
                qk_banks.append(qk_ps)
                for i in range(2):
                    t = 2 * pair + i
                    for g in range(PASSES):
                        tokens = slice((t * PASSES + g) * P, (t * PASSES + g + 1) * P)
                        for acc, cols in ((qk_ps[:, i, :], QK_COLS), (v_ps[:, t, :], V_COLS)):
                            nc.tensor.matmul_mx(
                                out=acc,
                                lhsT=x_codes[:, tokens].bitcast(FP8X4),
                                lhsT_scale=x_scales[:, tokens],
                                rhs=w_codes[:, w_cols(g, cols)].bitcast(FP8X4),
                                rhs_scale=w_scales[:, w_cols(g, cols)],
                                start=(g == 0),
                                stop=(g == PASSES - 1),
                            )
            return qk_banks, v_ps

        def rotate(first_pos, qk_banks, v_ps, res_view, slot):
            sin_part = sin_pool.tile([P, 2 * NH, ROUND_TILES, HD], F32)
            for pair in range(ROUND_TILES // 2):
                x = qk_banks[pair][:].rearrange("p t (c d) -> p t c d", d=HD)
                js = slice(first_pos + 2 * pair, first_pos + 2 * pair + 2)
                ts = slice(2 * pair, 2 * pair + 2)
                nc.vector.tensor_tensor(
                    out=res_view[:, 0 : 2 * NH, slot + 2 * pair : slot + 2 * pair + 2, :].rearrange("p c t d -> p t c d"),
                    in0=cos_sb[:, js, :].unsqueeze(2).to_broadcast([P, 2, 2 * NH, HD]),
                    in1=x,
                    op=MULT,
                )
                for dst, src in ((slice(0, HALF), slice(HALF, HD)), (slice(HALF, HD), slice(0, HALF))):
                    nc.vector.tensor_tensor(
                        out=sin_part[:, :, ts, dst].rearrange("p c t d -> p t c d"),
                        in0=sin_sb[:, js, dst].unsqueeze(2).to_broadcast([P, 2, 2 * NH, HALF]),
                        in1=x[:, :, :, src],
                        op=MULT,
                    )
            rotated = res_view[:, 0 : 2 * NH, slot : slot + ROUND_TILES, :]
            nc.gpsimd.tensor_tensor(out=rotated, in0=rotated, in1=sin_part[:], op=ADD)
            nc.scalar.copy(
                out=res_view[:, 2 * NH : 3 * NH, slot : slot + ROUND_TILES, :],
                in_=v_ps[:].rearrange("p t (h d) -> p h t d", d=HD),
            )

        def store(b, first_pos, res_view):
            for which in range(3):
                rows = outs[which][b].rearrange("h (p j) d -> p h j d", j=POS)
                nc.sync.dma_start(
                    out=rows[:, :, first_pos : first_pos + STORE_TILES, :],
                    in_=res_view[:, which * NH : (which + 1) * NH, :, :],
                )

        grouped_rounds = {0: transpose_round(x_tiles[0]), 1: transpose_round(x_tiles[1])}
        quantised = {0: quantise_round(grouped_rounds[0])}
        res_view = None
        for r in range(ROUNDS):
            b, quarter = divmod(r, ROUNDS_PER_BATCH)
            first_pos = quarter * ROUND_TILES
            slot = first_pos % STORE_TILES
            if r + LOOKAHEAD < ROUNDS:
                x_tiles[r + LOOKAHEAD] = load_round(r + LOOKAHEAD)
            if r + 2 < ROUNDS:
                grouped_rounds[r + 2] = transpose_round(x_tiles[r + 2])
            if r + 1 < ROUNDS:
                quantised[r + 1] = quantise_round(grouped_rounds[r + 1])
            qk_banks, v_ps = multiply(quantised[r][0], quantised[r][1])
            if slot == 0:
                res = res_pool.tile([P, 3 * NH, STORE_TILES, HD], F32)
                res_view = res[:]
            rotate(first_pos, qk_banks, v_ps, res_view, slot)
            if slot + ROUND_TILES == STORE_TILES:
                store(b, first_pos + ROUND_TILES - STORE_TILES, res_view)
